import numpy as np
import ml_dtypes

BF16 = ml_dtypes.bfloat16


def bf(x):
    return np.asarray(x, np.float32).astype(BF16)


def f32(x):
    return np.asarray(x, np.float32)


def f64(x):
    return np.asarray(x).astype(np.float64)


def striped(idx):
    return np.tile(idx.reshape(-1, 16).T, (8, 1))


C, S, K, H, N = 384, 1024, 4, 512, 4096
SLOPE = 0.2


def setup_inputs():
    z = np.random.standard_normal((C, S))
    z = z - z.mean(axis=0, keepdims=True)
    z = z / np.sqrt((z * z).mean(axis=0, keepdims=True))
    idx = np.concatenate([np.random.permutation(S)[:H] for _ in range(N // H)])
    return {"x": f32(z), "w_knn": bf(np.random.standard_normal((C + C, C)) / np.sqrt(C)), "b_knn": f32(0.1 * np.random.standard_normal((C, 1))), "offs": striped(idx)}


def reference(x, w_knn, b_knn, offs):
    idx = offs[:16].T.reshape(-1)
    x = f64(x)
    w = f64(w_knn)
    d = x[:, idx] + np.tile(-x, (1, K))
    v = w[:C].T @ d + np.tile(w[C:].T @ x + f64(b_knn), (1, K))
    v = np.maximum(v, SLOPE * v)
    return v.reshape(C, K, S).max(axis=1)

@@ -1,0 +1,98 @@
+import concourse.mybir as mybir
+
+F32 = mybir.dt.float32
+BF16 = mybir.dt.bfloat16
+U16 = mybir.dt.uint16
+ADD = mybir.AluOpType.add
+MULT = mybir.AluOpType.mult
+MAX = mybir.AluOpType.max
+
+P = 128
+C = 384
+S = 1024
+K = 4
+N = K * S
+SLOPE = 0.2
+BLOCKS = C // P
+PIECE = 512
+CHUNKS = S // PIECE
+
+FLOPS = 2 * C * C * (N + S)
+
+
+def tile_pctransformer_kernel(tc, x, w_knn, b_knn, offs, out):
+    nc = tc.nc
+    with (
+        tc.tile_pool(name="held", bufs=1) as held,
+        tc.tile_pool(name="diff", bufs=6) as diff,
+        tc.tile_pool(name="work", bufs=2) as work,
+        tc.psum_pool(name="acc", bufs=2) as acc_pool,
+        tc.psum_pool(name="own", bufs=2) as own_pool,
+    ):
+        offsets = held.tile([P, N // 16], U16, name="offsets")
+        nc.sync.dma_start(offsets[:], offs)
+        x_f32 = [held.tile([P, S], F32, name=f"x_f32_{c}") for c in range(BLOCKS)]
+        for c in range(BLOCKS):
+            nc.sync.dma_start(x_f32[c][:], x[c * P : (c + 1) * P, :])
+        w_diff = held.tile([P, BLOCKS, C], BF16, name="w_diff")
+        w_own = held.tile([P, BLOCKS, C], BF16, name="w_own")
+        nc.gpsimd.dma_start(w_diff[:], w_knn[0:C, :].rearrange("(c p) m -> p c m", p=P))
+        nc.gpsimd.dma_start(w_own[:], w_knn[C : 2 * C, :].rearrange("(c p) m -> p c m", p=P))
+        bias = held.tile([P, BLOCKS], F32, name="bias")
+        with nc.allow_non_contiguous_dma(reason="384 bias values, one to a partition"):
+            nc.gpsimd.dma_start(bias[:], b_knn.rearrange("(m p) o -> p (m o)", p=P))
+
+        x_neg = [held.tile([P, S], F32, name=f"x_neg_{c}") for c in range(BLOCKS)]
+        x_bf = [held.tile([P, S], BF16, name=f"x_bf_{c}") for c in range(BLOCKS)]
+        for chunk in range(CHUNKS):
+            cols = slice(chunk * PIECE, (chunk + 1) * PIECE)
+            for c in range(BLOCKS):
+                nc.scalar.mul(x_neg[c][:, cols], x_f32[c][:, cols], -1.0)
+        for c in range(BLOCKS):
+            nc.scalar.copy(x_bf[c][:], x_f32[c][:])
+
+        for chunk in range(CHUNKS):
+            cols = slice(chunk * PIECE, (chunk + 1) * PIECE)
+            best = [work.tile([P, PIECE], F32, name=f"best{m}") for m in range(BLOCKS)]
+            for k in range(K):
+                first = (k * S + chunk * PIECE) // 16
+                acc = [acc_pool.tile([P, PIECE], F32, name=f"acc{m}") for m in range(BLOCKS)]
+                for c in range(BLOCKS):
+                    d_f32 = diff.tile([P, PIECE], F32, name="d_f32")
+                    nc.vector.tensor_tensor(
+                        d_f32[:],
+                        x_f32[c][:].indirect(offsets[:, first : first + PIECE // 16]),
+                        x_neg[c][:, cols],
+                        ADD,
+                    )
+                    d_bf = diff.tile([P, PIECE], BF16, name="d_bf")
+                    nc.scalar.copy(d_bf[:], d_f32[:])
+                    for m in range(BLOCKS):
+                        nc.tensor.matmul(
+                            acc[m][:],
+                            w_diff[:, c, m * P : (m + 1) * P],
+                            d_bf[:],
+                            start=(c == 0),
+                            stop=(c == BLOCKS - 1),
+                        )
+                for m in range(BLOCKS):
+                    if k == 0:
+                        nc.scalar.copy(best[m][:], acc[m][:])
+                    else:
+                        nc.vector.tensor_tensor(best[m][:], acc[m][:], best[m][:], MAX)
+
+            for m in range(BLOCKS):
+                own = own_pool.tile([P, PIECE], F32, name="own")
+                for c in range(BLOCKS):
+                    nc.tensor.matmul(
+                        own[:],
+                        w_own[:, c, m * P : (m + 1) * P],
+                        x_bf[c][:, cols],
+                        start=(c == 0),
+                        stop=(c == BLOCKS - 1),
+                    )
+                v_max = work.tile([P, PIECE], F32, name="v_max")
+                nc.vector.scalar_tensor_tensor(v_max[:], own[:], bias[:, m : m + 1], best[m][:], ADD, ADD)
+                result = work.tile([P, PIECE], F32, name="result")
+                nc.vector.scalar_tensor_tensor(result[:], v_max[:], SLOPE, v_max[:], MULT, MAX)
+                nc.sync.dma_start(out[m * P : (m + 1) * P, cols], result[:])

@@ -36,51 +36,53 @@ def tile_pctransformer_kernel(tc, x, w_knn, b_knn, offs, out):
             nc.sync.dma_start(x_f32[c][:], x[c * P : (c + 1) * P, :])
         w_diff = held.tile([P, BLOCKS, C], BF16, name="w_diff")
         w_own = held.tile([P, BLOCKS, C], BF16, name="w_own")
-        nc.gpsimd.dma_start(w_diff[:], w_knn[0:C, :].rearrange("(c p) m -> p c m", p=P))
-        nc.gpsimd.dma_start(w_own[:], w_knn[C : 2 * C, :].rearrange("(c p) m -> p c m", p=P))
+        nc.sync.dma_start(w_diff[:], w_knn[0:C, :].rearrange("(c p) m -> p c m", p=P))
+        nc.sync.dma_start(w_own[:], w_knn[C : 2 * C, :].rearrange("(c p) m -> p c m", p=P))
         bias = held.tile([P, BLOCKS], F32, name="bias")
         with nc.allow_non_contiguous_dma(reason="384 bias values, one to a partition"):
-            nc.gpsimd.dma_start(bias[:], b_knn.rearrange("(m p) o -> p (m o)", p=P))
+            nc.sync.dma_start(bias[:], b_knn.rearrange("(m p) o -> p (m o)", p=P))
 
         x_neg = [held.tile([P, S], F32, name=f"x_neg_{c}") for c in range(BLOCKS)]
         x_bf = [held.tile([P, S], BF16, name=f"x_bf_{c}") for c in range(BLOCKS)]
-        for chunk in range(CHUNKS):
+        best = [[held.tile([P, PIECE], F32, name=f"best{chunk}_{m}") for m in range(BLOCKS)] for chunk in range(CHUNKS)]
+
+        def products(chunk, k):
+            cols = slice(chunk * PIECE, (chunk + 1) * PIECE)
+            first = (k * S + chunk * PIECE) // 16
+            acc = [acc_pool.tile([P, PIECE], F32, name=f"acc{m}") for m in range(BLOCKS)]
+            for c in range(BLOCKS):
+                if k == 0:
+                    nc.scalar.mul(x_neg[c][:, cols], x_f32[c][:, cols], -1.0)
+                d_f32 = diff.tile([P, PIECE], F32, name="d_f32")
+                nc.vector.tensor_tensor(
+                    d_f32[:],
+                    x_f32[c][:].indirect(offsets[:, first : first + PIECE // 16]),
+                    x_neg[c][:, cols],
+                    ADD,
+                )
+                d_bf = diff.tile([P, PIECE], BF16, name="d_bf")
+                nc.scalar.copy(d_bf[:], d_f32[:])
+                for m in range(BLOCKS):
+                    nc.tensor.matmul(
+                        acc[m][:],
+                        w_diff[:, c, m * P : (m + 1) * P],
+                        d_bf[:],
+                        start=(c == 0),
+                        stop=(c == BLOCKS - 1),
+                    )
+            return acc
+
+        def fold(chunk, k, acc):
+            for m in range(BLOCKS):
+                if k == 0:
+                    nc.scalar.copy(best[chunk][m][:], acc[m][:])
+                else:
+                    nc.vector.tensor_tensor(best[chunk][m][:], acc[m][:], best[chunk][m][:], MAX)
+
+        def finish(chunk):
             cols = slice(chunk * PIECE, (chunk + 1) * PIECE)
             for c in range(BLOCKS):
-                nc.scalar.mul(x_neg[c][:, cols], x_f32[c][:, cols], -1.0)
-        for c in range(BLOCKS):
-            nc.scalar.copy(x_bf[c][:], x_f32[c][:])
-
-        for chunk in range(CHUNKS):
-            cols = slice(chunk * PIECE, (chunk + 1) * PIECE)
-            best = [work.tile([P, PIECE], F32, name=f"best{m}") for m in range(BLOCKS)]
-            for k in range(K):
-                first = (k * S + chunk * PIECE) // 16
-                acc = [acc_pool.tile([P, PIECE], F32, name=f"acc{m}") for m in range(BLOCKS)]
-                for c in range(BLOCKS):
-                    d_f32 = diff.tile([P, PIECE], F32, name="d_f32")
-                    nc.vector.tensor_tensor(
-                        d_f32[:],
-                        x_f32[c][:].indirect(offsets[:, first : first + PIECE // 16]),
-                        x_neg[c][:, cols],
-                        ADD,
-                    )
-                    d_bf = diff.tile([P, PIECE], BF16, name="d_bf")
-                    nc.scalar.copy(d_bf[:], d_f32[:])
-                    for m in range(BLOCKS):
-                        nc.tensor.matmul(
-                            acc[m][:],
-                            w_diff[:, c, m * P : (m + 1) * P],
-                            d_bf[:],
-                            start=(c == 0),
-                            stop=(c == BLOCKS - 1),
-                        )
-                for m in range(BLOCKS):
-                    if k == 0:
-                        nc.scalar.copy(best[m][:], acc[m][:])
-                    else:
-                        nc.vector.tensor_tensor(best[m][:], acc[m][:], best[m][:], MAX)
-
+                nc.scalar.copy(x_bf[c][:, cols], x_f32[c][:, cols])
             for m in range(BLOCKS):
                 own = own_pool.tile([P, PIECE], F32, name="own")
                 for c in range(BLOCKS):
@@ -92,7 +94,19 @@ def tile_pctransformer_kernel(tc, x, w_knn, b_knn, offs, out):
                         stop=(c == BLOCKS - 1),
                     )
                 v_max = work.tile([P, PIECE], F32, name="v_max")
-                nc.vector.scalar_tensor_tensor(v_max[:], own[:], bias[:, m : m + 1], best[m][:], ADD, ADD)
+                nc.vector.scalar_tensor_tensor(v_max[:], own[:], bias[:, m : m + 1], best[chunk][m][:], ADD, ADD)
                 result = work.tile([P, PIECE], F32, name="result")
                 nc.vector.scalar_tensor_tensor(result[:], v_max[:], SLOPE, v_max[:], MULT, MAX)
                 nc.sync.dma_start(out[m * P : (m + 1) * P, cols], result[:])
+
+        unfolded = None
+        for chunk in range(CHUNKS):
+            for k in range(K):
+                acc = products(chunk, k)
+                if unfolded is not None:
+                    fold(*unfolded)
+                unfolded = (chunk, k, acc)
+            if chunk > 0:
+                finish(chunk - 1)
+        fold(*unfolded)
+        finish(CHUNKS - 1)

@@ -6,6 +6,7 @@ U16 = mybir.dt.uint16
 ADD = mybir.AluOpType.add
 MULT = mybir.AluOpType.mult
 MAX = mybir.AluOpType.max
+IDENTITY = mybir.ActivationFunctionType.Identity
 
 P = 128
 C = 384
@@ -25,7 +26,7 @@ def tile_pctransformer_kernel(tc, x, w_knn, b_knn, offs, out):
     with (
         tc.tile_pool(name="held", bufs=1) as held,
         tc.tile_pool(name="diff", bufs=6) as diff,
-        tc.tile_pool(name="work", bufs=2) as work,
+        tc.tile_pool(name="work", bufs=BLOCKS) as work,
         tc.psum_pool(name="acc", bufs=2) as acc_pool,
         tc.psum_pool(name="own", bufs=2) as own_pool,
     ):
@@ -45,6 +46,8 @@ def tile_pctransformer_kernel(tc, x, w_knn, b_knn, offs, out):
         x_neg = [held.tile([P, S], F32, name=f"x_neg_{c}") for c in range(BLOCKS)]
         x_bf = [held.tile([P, S], BF16, name=f"x_bf_{c}") for c in range(BLOCKS)]
         best = [[held.tile([P, PIECE], F32, name=f"best{chunk}_{m}") for m in range(BLOCKS)] for chunk in range(CHUNKS)]
+
+        own = [[held.tile([P, PIECE], F32, name=f"own{chunk}_{m}") for m in range(BLOCKS)] for chunk in range(CHUNKS)]
 
         def products(chunk, k):
             cols = slice(chunk * PIECE, (chunk + 1) * PIECE)
@@ -79,24 +82,30 @@ def tile_pctransformer_kernel(tc, x, w_knn, b_knn, offs, out):
                 else:
                     nc.vector.tensor_tensor(best[chunk][m][:], acc[m][:], best[chunk][m][:], MAX)
 
-        def finish(chunk):
+        def own_term(chunk):
             cols = slice(chunk * PIECE, (chunk + 1) * PIECE)
             for c in range(BLOCKS):
                 nc.scalar.copy(x_bf[c][:, cols], x_f32[c][:, cols])
             for m in range(BLOCKS):
-                own = own_pool.tile([P, PIECE], F32, name="own")
+                own_ps = own_pool.tile([P, PIECE], F32, name="own_ps")
                 for c in range(BLOCKS):
                     nc.tensor.matmul(
-                        own[:],
+                        own_ps[:],
                         w_own[:, c, m * P : (m + 1) * P],
                         x_bf[c][:, cols],
                         start=(c == 0),
                         stop=(c == BLOCKS - 1),
                     )
-                v_max = work.tile([P, PIECE], F32, name="v_max")
-                nc.vector.scalar_tensor_tensor(v_max[:], own[:], bias[:, m : m + 1], best[chunk][m][:], ADD, ADD)
+                nc.scalar.activation(own[chunk][m][:], own_ps[:], IDENTITY, bias=bias[:, m : m + 1])
+
+        def finish(chunk):
+            cols = slice(chunk * PIECE, (chunk + 1) * PIECE)
+            v_max = [work.tile([P, PIECE], F32, name="v_max") for m in range(BLOCKS)]
+            for m in range(BLOCKS):
+                nc.vector.tensor_tensor(v_max[m][:], best[chunk][m][:], own[chunk][m][:], ADD)
+            for m in range(BLOCKS):
                 result = work.tile([P, PIECE], F32, name="result")
-                nc.vector.scalar_tensor_tensor(result[:], v_max[:], SLOPE, v_max[:], MULT, MAX)
+                nc.vector.scalar_tensor_tensor(result[:], v_max[m][:], SLOPE, v_max[m][:], MULT, MAX)
                 nc.sync.dma_start(out[m * P : (m + 1) * P, cols], result[:])
 
         unfolded = None
@@ -106,6 +115,7 @@ def tile_pctransformer_kernel(tc, x, w_knn, b_knn, offs, out):
                 if unfolded is not None:
                     fold(*unfolded)
                 unfolded = (chunk, k, acc)
+            own_term(chunk)
             if chunk > 0:
                 finish(chunk - 1)
         fold(*unfolded)

@@ -1,4 +1,5 @@
 import concourse.mybir as mybir
+from concourse.masks import make_identity
 
 F32 = mybir.dt.float32
 BF16 = mybir.dt.bfloat16
@@ -17,6 +18,7 @@ SLOPE = 0.2
 BLOCKS = C // P
 PIECE = 512
 CHUNKS = S // PIECE
+BANKS = 8
 
 FLOPS = 2 * C * C * (N + S)
 
@@ -25,10 +27,9 @@ def tile_pctransformer_kernel(tc, x, w_knn, b_knn, offs, out):
     nc = tc.nc
     with (
         tc.tile_pool(name="held", bufs=1) as held,
-        tc.tile_pool(name="diff", bufs=6) as diff,
-        tc.tile_pool(name="work", bufs=BLOCKS) as work,
-        tc.psum_pool(name="acc", bufs=2) as acc_pool,
-        tc.psum_pool(name="own", bufs=2) as own_pool,
+        tc.tile_pool(name="diff", bufs=4) as diff,
+        tc.tile_pool(name="work", bufs=CHUNKS * BLOCKS) as work,
+        tc.psum_pool(name="psum", bufs=1) as psum,
     ):
         offsets = held.tile([P, N // 16], U16, name="offsets")
         nc.sync.dma_start(offsets[:], offs)
@@ -42,17 +43,20 @@ def tile_pctransformer_kernel(tc, x, w_knn, b_knn, offs, out):
         bias = held.tile([P, BLOCKS], F32, name="bias")
         with nc.allow_non_contiguous_dma(reason="384 bias values, one to a partition"):
             nc.sync.dma_start(bias[:], b_knn.rearrange("(m p) o -> p (m o)", p=P))
+        identity = held.tile([P, P], F32, name="identity")
+        make_identity(nc, identity[:])
 
         x_neg = [held.tile([P, S], F32, name=f"x_neg_{c}") for c in range(BLOCKS)]
         x_bf = [held.tile([P, S], BF16, name=f"x_bf_{c}") for c in range(BLOCKS)]
         best = [[held.tile([P, PIECE], F32, name=f"best{chunk}_{m}") for m in range(BLOCKS)] for chunk in range(CHUNKS)]
+        v_max = [[held.tile([P, PIECE], F32, name=f"v_max{chunk}_{m}") for m in range(BLOCKS)] for chunk in range(CHUNKS)]
 
-        own = [[held.tile([P, PIECE], F32, name=f"own{chunk}_{m}") for m in range(BLOCKS)] for chunk in range(CHUNKS)]
+        free_banks = [psum.tile([P, PIECE], F32, name=f"bank{b}") for b in range(BANKS)]
 
         def products(chunk, k):
             cols = slice(chunk * PIECE, (chunk + 1) * PIECE)
             first = (k * S + chunk * PIECE) // 16
-            acc = [acc_pool.tile([P, PIECE], F32, name=f"acc{m}") for m in range(BLOCKS)]
+            acc = [free_banks.pop(0) for m in range(BLOCKS)]
             for c in range(BLOCKS):
                 if k == 0:
                     nc.scalar.mul(x_neg[c][:, cols], x_f32[c][:, cols], -1.0)
@@ -81,31 +85,48 @@ def tile_pctransformer_kernel(tc, x, w_knn, b_knn, offs, out):
                     nc.scalar.copy(best[chunk][m][:], acc[m][:])
                 else:
                     nc.vector.tensor_tensor(best[chunk][m][:], acc[m][:], best[chunk][m][:], MAX)
+            free_banks.extend(acc)
 
-        def own_term(chunk):
+        def summed_in_psum(chunk, m):
+            return chunk < CHUNKS - 1 or m == 0
+
+        def own_term(chunk, m, closed):
+            cols = slice(chunk * PIECE, (chunk + 1) * PIECE)
+            bank = free_banks.pop(0)
+            for c in range(BLOCKS):
+                nc.tensor.matmul(
+                    bank[:],
+                    w_own[:, c, m * P : (m + 1) * P],
+                    x_bf[c][:, cols],
+                    start=(c == 0),
+                    stop=(closed and c == BLOCKS - 1),
+                )
+            return bank
+
+        def take_out(chunk, m, bank):
+            nc.scalar.activation(v_max[chunk][m][:], bank[:], IDENTITY, bias=bias[:, m : m + 1])
+            free_banks.append(bank)
+
+        def prepare(chunk):
             cols = slice(chunk * PIECE, (chunk + 1) * PIECE)
             for c in range(BLOCKS):
                 nc.scalar.copy(x_bf[c][:, cols], x_f32[c][:, cols])
             for m in range(BLOCKS):
-                own_ps = own_pool.tile([P, PIECE], F32, name="own_ps")
-                for c in range(BLOCKS):
-                    nc.tensor.matmul(
-                        own_ps[:],
-                        w_own[:, c, m * P : (m + 1) * P],
-                        x_bf[c][:, cols],
-                        start=(c == 0),
-                        stop=(c == BLOCKS - 1),
-                    )
-                nc.scalar.activation(own[chunk][m][:], own_ps[:], IDENTITY, bias=bias[:, m : m + 1])
+                if not summed_in_psum(chunk, m):
+                    take_out(chunk, m, own_term(chunk, m, closed=True))
 
         def finish(chunk):
             cols = slice(chunk * PIECE, (chunk + 1) * PIECE)
-            v_max = [work.tile([P, PIECE], F32, name="v_max") for m in range(BLOCKS)]
             for m in range(BLOCKS):
-                nc.vector.tensor_tensor(v_max[m][:], best[chunk][m][:], own[chunk][m][:], ADD)
+                if summed_in_psum(chunk, m):
+                    bank = own_term(chunk, m, closed=False)
+                    nc.tensor.matmul(bank[:], identity[:], best[chunk][m][:], start=False, stop=True)
+                    take_out(chunk, m, bank)
+                else:
+                    nc.vector.tensor_tensor(v_max[chunk][m][:], best[chunk][m][:], v_max[chunk][m][:], ADD)
             for m in range(BLOCKS):
                 result = work.tile([P, PIECE], F32, name="result")
-                nc.vector.scalar_tensor_tensor(result[:], v_max[m][:], SLOPE, v_max[m][:], MULT, MAX)
+                nc.vector.scalar_tensor_tensor(result[:], v_max[chunk][m][:], SLOPE, v_max[chunk][m][:], MULT, MAX)
                 nc.sync.dma_start(out[m * P : (m + 1) * P, cols], result[:])
 
         unfolded = None
@@ -114,9 +135,10 @@ def tile_pctransformer_kernel(tc, x, w_knn, b_knn, offs, out):
                 acc = products(chunk, k)
                 if unfolded is not None:
                     fold(*unfolded)
+                    if k == 0:
+                        finish(chunk - 1)
                 unfolded = (chunk, k, acc)
-            own_term(chunk)
-            if chunk > 0:
-                finish(chunk - 1)
+                if k == 1:
+                    prepare(chunk)
         fold(*unfolded)
         finish(CHUNKS - 1)

@@ -8,6 +8,7 @@ ADD = mybir.AluOpType.add
 MULT = mybir.AluOpType.mult
 MAX = mybir.AluOpType.max
 IDENTITY = mybir.ActivationFunctionType.Identity
+RELU = mybir.ActivationFunctionType.Relu
 
 P = 128
 C = 384
@@ -27,7 +28,7 @@ def tile_pctransformer_kernel(tc, x, w_knn, b_knn, offs, out):
     nc = tc.nc
     with (
         tc.tile_pool(name="held", bufs=1) as held,
-        tc.tile_pool(name="diff", bufs=4) as diff,
+        tc.tile_pool(name="diff", bufs=5) as diff,
         tc.tile_pool(name="work", bufs=CHUNKS * BLOCKS) as work,
         tc.psum_pool(name="psum", bufs=1) as psum,
     ):
@@ -46,10 +47,15 @@ def tile_pctransformer_kernel(tc, x, w_knn, b_knn, offs, out):
         identity = held.tile([P, P], F32, name="identity")
         make_identity(nc, identity[:])
 
+        bias_low = held.tile([P, BLOCKS], F32, name="bias_low")
+        bias_high = held.tile([P, BLOCKS], F32, name="bias_high")
+        nc.scalar.mul(bias_low[:], bias[:], SLOPE)
+        nc.scalar.mul(bias_high[:], bias[:], 1.0 - SLOPE)
+
         x_neg = [held.tile([P, S], F32, name=f"x_neg_{c}") for c in range(BLOCKS)]
         x_bf = [held.tile([P, S], BF16, name=f"x_bf_{c}") for c in range(BLOCKS)]
         best = [[held.tile([P, PIECE], F32, name=f"best{chunk}_{m}") for m in range(BLOCKS)] for chunk in range(CHUNKS)]
-        v_max = [[held.tile([P, PIECE], F32, name=f"v_max{chunk}_{m}") for m in range(BLOCKS)] for chunk in range(CHUNKS)]
+        v_max = [held.tile([P, PIECE], F32, name=f"v_max_{m}") for m in range(BLOCKS)]
 
         free_banks = [psum.tile([P, PIECE], F32, name=f"bank{b}") for b in range(BANKS)]
 
@@ -87,8 +93,6 @@ def tile_pctransformer_kernel(tc, x, w_knn, b_knn, offs, out):
                     nc.vector.tensor_tensor(best[chunk][m][:], acc[m][:], best[chunk][m][:], MAX)
             free_banks.extend(acc)
 
-        def summed_in_psum(chunk, m):
-            return chunk < CHUNKS - 1 or m == 0
 
         def own_term(chunk, m, closed):
             cols = slice(chunk * PIECE, (chunk + 1) * PIECE)
@@ -103,42 +107,54 @@ def tile_pctransformer_kernel(tc, x, w_knn, b_knn, offs, out):
                 )
             return bank
 
-        def take_out(chunk, m, bank):
-            nc.scalar.activation(v_max[chunk][m][:], bank[:], IDENTITY, bias=bias[:, m : m + 1])
+        def sum_in_psum(chunk, m):
+            bank = own_term(chunk, m, closed=False)
+            nc.tensor.matmul(bank[:], identity[:], best[chunk][m][:], start=False, stop=True)
+            return bank
+
+        def take_out(m, bank):
+            nc.scalar.activation(v_max[m][:], bank[:], IDENTITY, bias=bias[:, m : m + 1])
             free_banks.append(bank)
 
-        def prepare(chunk):
-            cols = slice(chunk * PIECE, (chunk + 1) * PIECE)
+        def prepare():
             for c in range(BLOCKS):
-                nc.scalar.copy(x_bf[c][:, cols], x_f32[c][:, cols])
-            for m in range(BLOCKS):
-                if not summed_in_psum(chunk, m):
-                    take_out(chunk, m, own_term(chunk, m, closed=True))
+                nc.scalar.copy(x_bf[c][:], x_f32[c][:])
+            for m in range(1, BLOCKS):
+                take_out(m, own_term(CHUNKS - 1, m, closed=True))
 
-        def finish(chunk):
+        def finish_without_vector(chunk):
             cols = slice(chunk * PIECE, (chunk + 1) * PIECE)
             for m in range(BLOCKS):
-                if summed_in_psum(chunk, m):
-                    bank = own_term(chunk, m, closed=False)
-                    nc.tensor.matmul(bank[:], identity[:], best[chunk][m][:], start=False, stop=True)
-                    take_out(chunk, m, bank)
-                else:
-                    nc.vector.tensor_tensor(v_max[chunk][m][:], best[chunk][m][:], v_max[chunk][m][:], ADD)
+                bank = sum_in_psum(chunk, m)
+                low = work.tile([P, PIECE], F32, name="low")
+                high = work.tile([P, PIECE], F32, name="high")
+                nc.scalar.activation(low[:], bank[:], IDENTITY, bias=bias_low[:, m : m + 1], scale=SLOPE)
+                nc.scalar.activation(high[:], bank[:], RELU, bias=bias_high[:, m : m + 1], scale=1.0 - SLOPE)
+                free_banks.append(bank)
+                result = work.tile([P, PIECE], F32, name="result")
+                nc.gpsimd.tensor_tensor(result[:], low[:], high[:], ADD)
+                nc.sync.dma_start(out[m * P : (m + 1) * P, cols], result[:])
+
+        def finish_last_chunk(chunk):
+            cols = slice(chunk * PIECE, (chunk + 1) * PIECE)
+            take_out(0, sum_in_psum(chunk, 0))
+            for m in range(1, BLOCKS):
+                nc.vector.tensor_tensor(v_max[m][:], best[chunk][m][:], v_max[m][:], ADD)
             for m in range(BLOCKS):
                 result = work.tile([P, PIECE], F32, name="result")
-                nc.vector.scalar_tensor_tensor(result[:], v_max[chunk][m][:], SLOPE, v_max[chunk][m][:], MULT, MAX)
+                nc.vector.scalar_tensor_tensor(result[:], v_max[m][:], SLOPE, v_max[m][:], MULT, MAX)
                 nc.sync.dma_start(out[m * P : (m + 1) * P, cols], result[:])
 
         unfolded = None
         for chunk in range(CHUNKS):
             for k in range(K):
                 acc = products(chunk, k)
-                if unfolded is not None:
+                if unfolded is None:
+                    prepare()
+                else:
                     fold(*unfolded)
                     if k == 0:
-                        finish(chunk - 1)
+                        finish_without_vector(chunk - 1)
                 unfolded = (chunk, k, acc)
-                if k == 1:
-                    prepare(chunk)
         fold(*unfolded)
-        finish(CHUNKS - 1)
+        finish_last_chunk(CHUNKS - 1)

@@ -28,7 +28,7 @@ def tile_pctransformer_kernel(tc, x, w_knn, b_knn, offs, out):
     nc = tc.nc
     with (
         tc.tile_pool(name="held", bufs=1) as held,
-        tc.tile_pool(name="diff", bufs=5) as diff,
+        tc.tile_pool(name="diff", bufs=6) as diff,
         tc.tile_pool(name="work", bufs=CHUNKS * BLOCKS) as work,
         tc.psum_pool(name="psum", bufs=1) as psum,
     ):
@@ -122,25 +122,24 @@ def tile_pctransformer_kernel(tc, x, w_knn, b_knn, offs, out):
             for m in range(1, BLOCKS):
                 take_out(m, own_term(CHUNKS - 1, m, closed=True))
 
-        def finish_without_vector(chunk):
+        def finish_without_vector(chunk, m):
             cols = slice(chunk * PIECE, (chunk + 1) * PIECE)
-            for m in range(BLOCKS):
-                bank = sum_in_psum(chunk, m)
-                low = work.tile([P, PIECE], F32, name="low")
-                high = work.tile([P, PIECE], F32, name="high")
-                nc.scalar.activation(low[:], bank[:], IDENTITY, bias=bias_low[:, m : m + 1], scale=SLOPE)
-                nc.scalar.activation(high[:], bank[:], RELU, bias=bias_high[:, m : m + 1], scale=1.0 - SLOPE)
-                free_banks.append(bank)
-                result = work.tile([P, PIECE], F32, name="result")
-                nc.gpsimd.tensor_tensor(result[:], low[:], high[:], ADD)
-                nc.sync.dma_start(out[m * P : (m + 1) * P, cols], result[:])
+            bank = sum_in_psum(chunk, m)
+            low = work.tile([P, PIECE], F32, name="low")
+            high = work.tile([P, PIECE], F32, name="high")
+            nc.scalar.activation(low[:], bank[:], IDENTITY, bias=bias_low[:, m : m + 1], scale=SLOPE)
+            nc.scalar.activation(high[:], bank[:], RELU, bias=bias_high[:, m : m + 1], scale=1.0 - SLOPE)
+            free_banks.append(bank)
+            result = work.tile([P, PIECE], F32, name="result")
+            nc.gpsimd.tensor_tensor(result[:], low[:], high[:], ADD)
+            nc.sync.dma_start(out[m * P : (m + 1) * P, cols], result[:])
 
         def finish_last_chunk(chunk):
             cols = slice(chunk * PIECE, (chunk + 1) * PIECE)
             take_out(0, sum_in_psum(chunk, 0))
             for m in range(1, BLOCKS):
                 nc.vector.tensor_tensor(v_max[m][:], best[chunk][m][:], v_max[m][:], ADD)
-            for m in range(BLOCKS):
+            for m in (1, 2, 0):
                 result = work.tile([P, PIECE], F32, name="result")
                 nc.vector.scalar_tensor_tensor(result[:], v_max[m][:], SLOPE, v_max[m][:], MULT, MAX)
                 nc.sync.dma_start(out[m * P : (m + 1) * P, cols], result[:])
@@ -153,8 +152,8 @@ def tile_pctransformer_kernel(tc, x, w_knn, b_knn, offs, out):
                     prepare()
                 else:
                     fold(*unfolded)
-                    if k == 0:
-                        finish_without_vector(chunk - 1)
+                if chunk > 0 and k < BLOCKS:
+                    finish_without_vector(chunk - 1, k)
                 unfolded = (chunk, k, acc)
         fold(*unfolded)
         finish_last_chunk(CHUNKS - 1)

@@ -140,9 +140,12 @@ def tile_pctransformer_kernel(tc, x, w_knn, b_knn, offs, out):
             for m in range(1, BLOCKS):
                 nc.vector.tensor_tensor(v_max[m][:], best[chunk][m][:], v_max[m][:], ADD)
             for m in (1, 2, 0):
-                result = work.tile([P, PIECE], F32, name="result")
-                nc.vector.scalar_tensor_tensor(result[:], v_max[m][:], SLOPE, v_max[m][:], MULT, MAX)
-                nc.sync.dma_start(out[m * P : (m + 1) * P, cols], result[:])
+                for half in range(0, PIECE, PIECE // 2):
+                    part = slice(half, half + PIECE // 2)
+                    result = work.tile([P, PIECE // 2], F32, name="half_result")
+                    nc.vector.scalar_tensor_tensor(result[:], v_max[m][:, part], SLOPE, v_max[m][:, part], MULT, MAX)
+                    first = chunk * PIECE + half
+                    nc.sync.dma_start(out[m * P : (m + 1) * P, first : first + PIECE // 2], result[:])
 
         unfolded = None
         for chunk in range(CHUNKS):

@@ -35,7 +35,8 @@ def tile_pctransformer_kernel(tc, x, w_knn, b_knn, offs, out):
         offsets = held.tile([P, N // 16], U16, name="offsets")
         nc.sync.dma_start(offsets[:], offs)
         x_f32 = [held.tile([P, S], F32, name=f"x_f32_{c}") for c in range(BLOCKS)]
-        for c in range(BLOCKS):
+        nc.scalar.dma_start(x_f32[0][:], x[0:P, :])
+        for c in range(1, BLOCKS):
             nc.sync.dma_start(x_f32[c][:], x[c * P : (c + 1) * P, :])
         w_diff = held.tile([P, BLOCKS, C], BF16, name="w_diff")
         w_own = held.tile([P, BLOCKS, C], BF16, name="w_own")

@@ -20,6 +20,7 @@ BLOCKS = C // P
 PIECE = 512
 CHUNKS = S // PIECE
 BANKS = 8
+LAST = CHUNKS - 1
 
 FLOPS = 2 * C * C * (N + S)
 
@@ -29,6 +30,7 @@ def tile_pctransformer_kernel(tc, x, w_knn, b_knn, offs, out):
     with (
         tc.tile_pool(name="held", bufs=1) as held,
         tc.tile_pool(name="diff", bufs=6) as diff,
+        tc.tile_pool(name="moving", bufs=4) as moving,
         tc.tile_pool(name="work", bufs=CHUNKS * BLOCKS) as work,
         tc.psum_pool(name="psum", bufs=1) as psum,
     ):
@@ -60,49 +62,89 @@ def tile_pctransformer_kernel(tc, x, w_knn, b_knn, offs, out):
 
         free_banks = [psum.tile([P, PIECE], F32, name=f"bank{b}") for b in range(BANKS)]
 
-        def products(chunk, k):
-            cols = slice(chunk * PIECE, (chunk + 1) * PIECE)
-            first = (k * S + chunk * PIECE) // 16
-            acc = [free_banks.pop(0) for m in range(BLOCKS)]
+        def columns(chunk):
+            return slice(chunk * PIECE, (chunk + 1) * PIECE)
+
+        def negate(chunk):
             for c in range(BLOCKS):
-                if k == 0:
-                    nc.scalar.mul(x_neg[c][:, cols], x_f32[c][:, cols], -1.0)
+                source, target = x_f32[c][:, columns(chunk)], x_neg[c][:, columns(chunk)]
+                if (chunk, c) == (0, 0):
+                    nc.vector.tensor_scalar_mul(target, source, -1.0)
+                else:
+                    nc.scalar.mul(target, source, -1.0)
+
+        def paired(chunk, m):
+            return (chunk, m) == (0, 0)
+
+        def products(chunk, k, d_first):
+            entry = (k * S + chunk * PIECE) // 16
+            banks = [free_banks.pop(0) for m in range(BLOCKS)]
+            subtracting = [m for m in range(BLOCKS) if k == 1 and paired(chunk, m)]
+            for m in subtracting:
+                for c in range(BLOCKS):
+                    nc.tensor.matmul(
+                        banks[m][:], w_diff[:, c, m * P : (m + 1) * P], d_first[c][:], start=(c == 0), stop=False
+                    )
+            d_piece = []
+            for c in range(BLOCKS):
                 d_f32 = diff.tile([P, PIECE], F32, name="d_f32")
                 nc.vector.tensor_tensor(
                     d_f32[:],
-                    x_f32[c][:].indirect(offsets[:, first : first + PIECE // 16]),
-                    x_neg[c][:, cols],
+                    x_f32[c][:].indirect(offsets[:, entry : entry + PIECE // 16]),
+                    x_neg[c][:, columns(chunk)],
                     ADD,
                 )
-                d_bf = diff.tile([P, PIECE], BF16, name="d_bf")
-                nc.scalar.copy(d_bf[:], d_f32[:])
+                d_bf = moving.tile([P, PIECE], BF16, name="d_bf")
+                nc.scalar.mul(d_bf[:], d_f32[:], -1.0 if subtracting else 1.0)
+                d_piece.append(d_bf)
                 for m in range(BLOCKS):
+                    stays_open = k == 0 and paired(chunk, m)
                     nc.tensor.matmul(
-                        acc[m][:],
+                        banks[m][:],
                         w_diff[:, c, m * P : (m + 1) * P],
                         d_bf[:],
-                        start=(c == 0),
-                        stop=(c == BLOCKS - 1),
+                        start=(c == 0 and m not in subtracting),
+                        stop=(c == BLOCKS - 1 and not stays_open),
                     )
-            return acc
+            return banks, d_piece
 
-        def fold(chunk, k, acc):
+        first_bank = {}
+
+        def fold(chunk, k, banks):
             for m in range(BLOCKS):
-                if k == 0:
-                    nc.scalar.copy(best[chunk][m][:], acc[m][:])
+                bank, running = banks[m], best[chunk][m]
+                if paired(chunk, m) and k < 3:
+                    if k == 0:
+                        first_bank[m] = bank
+                        continue
+                    if k == 1:
+                        gain = work.tile([P, PIECE], F32, name="gain")
+                        nc.scalar.activation(gain[:], bank[:], RELU, scale=-1.0)
+                        nc.tensor.matmul(first_bank[m][:], identity[:], gain[:], start=False, stop=True)
+                    if k == 2:
+                        nc.scalar.copy(running[:], bank[:])
+                        nc.vector.tensor_tensor(running[:], first_bank[m][:], running[:], MAX)
+                        free_banks.append(first_bank[m])
+                elif k == 0:
+                    nc.scalar.copy(running[:], bank[:])
+                elif k == 1 and chunk == 0:
+                    nc.vector.scalar_tensor_tensor(running[:], bank[:], -1.0, running[:], MULT, MAX)
                 else:
-                    nc.vector.tensor_tensor(best[chunk][m][:], acc[m][:], best[chunk][m][:], MAX)
-            free_banks.extend(acc)
+                    nc.vector.tensor_tensor(running[:], bank[:], running[:], MAX)
+                free_banks.append(bank)
 
+
+        def round_own(chunk):
+            for c in range(BLOCKS):
+                nc.scalar.copy(x_bf[c][:, columns(chunk)], x_f32[c][:, columns(chunk)])
 
         def own_term(chunk, m, closed):
-            cols = slice(chunk * PIECE, (chunk + 1) * PIECE)
             bank = free_banks.pop(0)
             for c in range(BLOCKS):
                 nc.tensor.matmul(
                     bank[:],
                     w_own[:, c, m * P : (m + 1) * P],
-                    x_bf[c][:, cols],
+                    x_bf[c][:, columns(chunk)],
                     start=(c == 0),
                     stop=(closed and c == BLOCKS - 1),
                 )
@@ -117,14 +159,7 @@ def tile_pctransformer_kernel(tc, x, w_knn, b_knn, offs, out):
             nc.scalar.activation(v_max[m][:], bank[:], IDENTITY, bias=bias[:, m : m + 1])
             free_banks.append(bank)
 
-        def prepare():
-            for c in range(BLOCKS):
-                nc.scalar.copy(x_bf[c][:], x_f32[c][:])
-            for m in range(1, BLOCKS):
-                take_out(m, own_term(CHUNKS - 1, m, closed=True))
-
         def finish_without_vector(chunk, m):
-            cols = slice(chunk * PIECE, (chunk + 1) * PIECE)
             bank = sum_in_psum(chunk, m)
             low = work.tile([P, PIECE], F32, name="low")
             high = work.tile([P, PIECE], F32, name="high")
@@ -133,31 +168,42 @@ def tile_pctransformer_kernel(tc, x, w_knn, b_knn, offs, out):
             free_banks.append(bank)
             result = work.tile([P, PIECE], F32, name="result")
             nc.gpsimd.tensor_tensor(result[:], low[:], high[:], ADD)
-            nc.sync.dma_start(out[m * P : (m + 1) * P, cols], result[:])
+            nc.sync.dma_start(out[m * P : (m + 1) * P, columns(chunk)], result[:])
 
-        def finish_last_chunk(chunk):
-            cols = slice(chunk * PIECE, (chunk + 1) * PIECE)
-            take_out(0, sum_in_psum(chunk, 0))
+        def finish_last_chunk():
+            take_out(0, sum_in_psum(LAST, 0))
             for m in range(1, BLOCKS):
-                nc.vector.tensor_tensor(v_max[m][:], best[chunk][m][:], v_max[m][:], ADD)
+                nc.vector.tensor_tensor(v_max[m][:], best[LAST][m][:], v_max[m][:], ADD)
             for m in (1, 2, 0):
                 for half in range(0, PIECE, PIECE // 2):
                     part = slice(half, half + PIECE // 2)
                     result = work.tile([P, PIECE // 2], F32, name="half_result")
                     nc.vector.scalar_tensor_tensor(result[:], v_max[m][:, part], SLOPE, v_max[m][:, part], MULT, MAX)
-                    first = chunk * PIECE + half
-                    nc.sync.dma_start(out[m * P : (m + 1) * P, first : first + PIECE // 2], result[:])
+                    left = LAST * PIECE + half
+                    nc.sync.dma_start(out[m * P : (m + 1) * P, left : left + PIECE // 2], result[:])
 
         unfolded = None
+        d_first = None
         for chunk in range(CHUNKS):
+            negate(chunk)
             for k in range(K):
-                acc = products(chunk, k)
-                if unfolded is None:
-                    prepare()
-                else:
+                banks, d_piece = products(chunk, k, d_first)
+                if k == 0:
+                    d_first = d_piece
+                if unfolded is not None:
                     fold(*unfolded)
-                if chunk > 0 and k < BLOCKS:
-                    finish_without_vector(chunk - 1, k)
-                unfolded = (chunk, k, acc)
+                if (chunk, k) == (0, 0):
+                    round_own(LAST)
+                    take_out(1, own_term(LAST, 1, closed=True))
+                if (chunk, k) == (0, 2):
+                    round_own(0)
+                if chunk == LAST and k == 0:
+                    finish_without_vector(0, 0)
+                    finish_without_vector(0, 1)
+                if chunk == LAST and k == 1:
+                    finish_without_vector(0, 2)
+                if (chunk, k) == (LAST, K - 1):
+                    take_out(2, own_term(LAST, 2, closed=True))
+                unfolded = (chunk, k, banks)
         fold(*unfolded)
-        finish_last_chunk(CHUNKS - 1)
+        finish_last_chunk()

@@ -34,10 +34,14 @@ def tile_pctransformer_kernel(tc, x, w_knn, b_knn, offs, out):
         tc.tile_pool(name="work", bufs=CHUNKS * BLOCKS) as work,
         tc.psum_pool(name="psum", bufs=1) as psum,
     ):
+        def columns(chunk):
+            return slice(chunk * PIECE, (chunk + 1) * PIECE)
+
         offsets = held.tile([P, N // 16], U16, name="offsets")
         nc.sync.dma_start(offsets[:], offs)
         x_f32 = [held.tile([P, S], F32, name=f"x_f32_{c}") for c in range(BLOCKS)]
-        nc.scalar.dma_start(x_f32[0][:], x[0:P, :])
+        nc.scalar.dma_start(x_f32[0][:, 0:PIECE], x[0:P, 0:PIECE])
+        nc.sync.dma_start(x_f32[0][:, PIECE:S], x[0:P, PIECE:S])
         for c in range(1, BLOCKS):
             nc.sync.dma_start(x_f32[c][:], x[c * P : (c + 1) * P, :])
         w_diff = held.tile([P, BLOCKS, C], BF16, name="w_diff")
@@ -62,16 +66,9 @@ def tile_pctransformer_kernel(tc, x, w_knn, b_knn, offs, out):
 
         free_banks = [psum.tile([P, PIECE], F32, name=f"bank{b}") for b in range(BANKS)]
 
-        def columns(chunk):
-            return slice(chunk * PIECE, (chunk + 1) * PIECE)
-
         def negate(chunk):
             for c in range(BLOCKS):
-                source, target = x_f32[c][:, columns(chunk)], x_neg[c][:, columns(chunk)]
-                if (chunk, c) == (0, 0):
-                    nc.vector.tensor_scalar_mul(target, source, -1.0)
-                else:
-                    nc.scalar.mul(target, source, -1.0)
+                nc.scalar.mul(x_neg[c][:, columns(chunk)], x_f32[c][:, columns(chunk)], -1.0)
 
         def paired(chunk, m):
             return (chunk, m) == (0, 0)

@@ -37,11 +37,11 @@ def tile_pctransformer_kernel(tc, x, w_knn, b_knn, offs, out):
         def columns(chunk):
             return slice(chunk * PIECE, (chunk + 1) * PIECE)
 
-        offsets = held.tile([P, N // 16], U16, name="offsets")
-        nc.sync.dma_start(offsets[:], offs)
         x_f32 = [held.tile([P, S], F32, name=f"x_f32_{c}") for c in range(BLOCKS)]
-        nc.scalar.dma_start(x_f32[0][:, 0:PIECE], x[0:P, 0:PIECE])
-        nc.sync.dma_start(x_f32[0][:, PIECE:S], x[0:P, PIECE:S])
+        offsets = held.tile([P, N // 16], U16, name="offsets")
+        for chunk in range(CHUNKS):
+            nc.sync.dma_start(x_f32[0][:, columns(chunk)], x[0:P, columns(chunk)])
+        nc.sync.dma_start(offsets[:], offs)
         for c in range(1, BLOCKS):
             nc.sync.dma_start(x_f32[c][:], x[c * P : (c + 1) * P, :])
         w_diff = held.tile([P, BLOCKS, C], BF16, name="w_diff")
@@ -53,11 +53,6 @@ def tile_pctransformer_kernel(tc, x, w_knn, b_knn, offs, out):
             nc.sync.dma_start(bias[:], b_knn.rearrange("(m p) o -> p (m o)", p=P))
         identity = held.tile([P, P], F32, name="identity")
         make_identity(nc, identity[:])
-
-        bias_low = held.tile([P, BLOCKS], F32, name="bias_low")
-        bias_high = held.tile([P, BLOCKS], F32, name="bias_high")
-        nc.scalar.mul(bias_low[:], bias[:], SLOPE)
-        nc.scalar.mul(bias_high[:], bias[:], 1.0 - SLOPE)
 
         x_neg = [held.tile([P, S], F32, name=f"x_neg_{c}") for c in range(BLOCKS)]
         x_bf = [held.tile([P, S], BF16, name=f"x_bf_{c}") for c in range(BLOCKS)]
@@ -73,37 +68,35 @@ def tile_pctransformer_kernel(tc, x, w_knn, b_knn, offs, out):
         def paired(chunk, m):
             return (chunk, m) == (0, 0)
 
-        def products(chunk, k, d_first):
-            entry = (k * S + chunk * PIECE) // 16
-            banks = [free_banks.pop(0) for m in range(BLOCKS)]
-            subtracting = [m for m in range(BLOCKS) if k == 1 and paired(chunk, m)]
-            for m in subtracting:
-                for c in range(BLOCKS):
-                    nc.tensor.matmul(
-                        banks[m][:], w_diff[:, c, m * P : (m + 1) * P], d_first[c][:], start=(c == 0), stop=False
-                    )
-            d_piece = []
+        def products(chunk, neighbours):
+            banks = {k: [free_banks.pop(0) for m in range(BLOCKS)] for k in neighbours}
             for c in range(BLOCKS):
-                d_f32 = diff.tile([P, PIECE], F32, name="d_f32")
-                nc.vector.tensor_tensor(
-                    d_f32[:],
-                    x_f32[c][:].indirect(offsets[:, entry : entry + PIECE // 16]),
-                    x_neg[c][:, columns(chunk)],
-                    ADD,
-                )
-                d_bf = moving.tile([P, PIECE], BF16, name="d_bf")
-                nc.scalar.mul(d_bf[:], d_f32[:], -1.0 if subtracting else 1.0)
-                d_piece.append(d_bf)
-                for m in range(BLOCKS):
-                    stays_open = k == 0 and paired(chunk, m)
-                    nc.tensor.matmul(
-                        banks[m][:],
-                        w_diff[:, c, m * P : (m + 1) * P],
-                        d_bf[:],
-                        start=(c == 0 and m not in subtracting),
-                        stop=(c == BLOCKS - 1 and not stays_open),
+                for k in neighbours:
+                    negated = (chunk, k) == (0, 1)
+                    entry = (k * S + chunk * PIECE) // 16
+                    d_f32 = diff.tile([P, PIECE], F32, name="d_f32")
+                    nc.vector.tensor_tensor(
+                        d_f32[:],
+                        x_f32[c][:].indirect(offsets[:, entry : entry + PIECE // 16]),
+                        x_neg[c][:, columns(chunk)],
+                        ADD,
                     )
-            return banks, d_piece
+                    d_bf = moving.tile([P, PIECE], BF16, name="d_bf")
+                    nc.scalar.mul(d_bf[:], d_f32[:], -1.0 if negated else 1.0)
+                    for m in range(BLOCKS):
+                        weights = w_diff[:, c, m * P : (m + 1) * P]
+                        stays_open = k == 0 and paired(chunk, m)
+                        is_open = negated and paired(chunk, m)
+                        nc.tensor.matmul(
+                            banks[k][m][:],
+                            weights,
+                            d_bf[:],
+                            start=(c == 0 and not is_open),
+                            stop=(c == BLOCKS - 1 and not stays_open),
+                        )
+                        if stays_open:
+                            nc.tensor.matmul(banks[1][m][:], weights, d_bf[:], start=(c == 0), stop=False)
+            return banks
 
         first_bank = {}
 
@@ -179,19 +172,22 @@ def tile_pctransformer_kernel(tc, x, w_knn, b_knn, offs, out):
                     left = LAST * PIECE + half
                     nc.sync.dma_start(out[m * P : (m + 1) * P, left : left + PIECE // 2], result[:])
 
-        unfolded = None
-        d_first = None
+        negate(0)
+        banks = products(0, (0, 1))
+        round_own(LAST)
+        fold(0, 0, banks[0])
+        take_out(1, own_term(LAST, 1, closed=True))
+        unfolded = (0, 1, banks[1])
+        bias_low = held.tile([P, BLOCKS], F32, name="bias_low")
+        bias_high = held.tile([P, BLOCKS], F32, name="bias_high")
+        nc.scalar.mul(bias_low[:], bias[:], SLOPE)
+        nc.scalar.mul(bias_high[:], bias[:], 1.0 - SLOPE)
         for chunk in range(CHUNKS):
-            negate(chunk)
-            for k in range(K):
-                banks, d_piece = products(chunk, k, d_first)
-                if k == 0:
-                    d_first = d_piece
-                if unfolded is not None:
-                    fold(*unfolded)
-                if (chunk, k) == (0, 0):
-                    round_own(LAST)
-                    take_out(1, own_term(LAST, 1, closed=True))
+            if chunk > 0:
+                negate(chunk)
+            for k in range(2 if chunk == 0 else 0, K):
+                banks = products(chunk, (k,))
+                fold(*unfolded)
                 if (chunk, k) == (0, 2):
                     round_own(0)
                 if chunk == LAST and k == 0:
@@ -201,6 +197,6 @@ def tile_pctransformer_kernel(tc, x, w_knn, b_knn, offs, out):
                     finish_without_vector(0, 2)
                 if (chunk, k) == (LAST, K - 1):
                     take_out(2, own_term(LAST, 2, closed=True))
-                unfolded = (chunk, k, banks)
+                unfolded = (chunk, k, banks[k])
         fold(*unfolded)
         finish_last_chunk()

@@ -46,8 +46,8 @@ def tile_pctransformer_kernel(tc, x, w_knn, b_knn, offs, out):
             nc.sync.dma_start(x_f32[c][:], x[c * P : (c + 1) * P, :])
         w_diff = held.tile([P, BLOCKS, C], BF16, name="w_diff")
         w_own = held.tile([P, BLOCKS, C], BF16, name="w_own")
-        nc.sync.dma_start(w_diff[:], w_knn[0:C, :].rearrange("(c p) m -> p c m", p=P))
         nc.sync.dma_start(w_own[:], w_knn[C : 2 * C, :].rearrange("(c p) m -> p c m", p=P))
+        nc.sync.dma_start(w_diff[:], w_knn[0:C, :].rearrange("(c p) m -> p c m", p=P))
         bias = held.tile([P, BLOCKS], F32, name="bias")
         with nc.allow_non_contiguous_dma(reason="384 bias values, one to a partition"):
             nc.sync.dma_start(bias[:], b_knn.rearrange("(m p) o -> p (m o)", p=P))
@@ -111,10 +111,10 @@ def tile_pctransformer_kernel(tc, x, w_knn, b_knn, offs, out):
                         gain = work.tile([P, PIECE], F32, name="gain")
                         nc.scalar.activation(gain[:], bank[:], RELU, scale=-1.0)
                         nc.tensor.matmul(first_bank[m][:], identity[:], gain[:], start=False, stop=True)
-                    if k == 2:
-                        nc.scalar.copy(running[:], bank[:])
-                        nc.vector.tensor_tensor(running[:], first_bank[m][:], running[:], MAX)
+                        nc.scalar.copy(running[:], first_bank[m][:])
                         free_banks.append(first_bank[m])
+                    if k == 2:
+                        nc.vector.tensor_tensor(running[:], bank[:], running[:], MAX)
                 elif k == 0:
                     nc.scalar.copy(running[:], bank[:])
                 elif k == 1 and chunk == 0:
@@ -173,10 +173,10 @@ def tile_pctransformer_kernel(tc, x, w_knn, b_knn, offs, out):
                     nc.sync.dma_start(out[m * P : (m + 1) * P, left : left + PIECE // 2], result[:])
 
         negate(0)
-        banks = products(0, (0, 1))
         round_own(LAST)
-        fold(0, 0, banks[0])
         take_out(1, own_term(LAST, 1, closed=True))
+        banks = products(0, (0, 1))
+        fold(0, 0, banks[0])
         unfolded = (0, 1, banks[1])
         bias_low = held.tile([P, BLOCKS], F32, name="bias_low")
         bias_high = held.tile([P, BLOCKS], F32, name="bias_high")

@@ -21,6 +21,7 @@ PIECE = 512
 CHUNKS = S // PIECE
 BANKS = 8
 LAST = CHUNKS - 1
+FIRST_FOLDED = (2, 0)
 
 FLOPS = 2 * C * C * (N + S)
 
@@ -63,10 +64,14 @@ def tile_pctransformer_kernel(tc, x, w_knn, b_knn, offs, out):
 
         def negate(chunk):
             for c in range(BLOCKS):
-                nc.scalar.mul(x_neg[c][:, columns(chunk)], x_f32[c][:, columns(chunk)], -1.0)
+                source, target = x_f32[c][:, columns(chunk)], x_neg[c][:, columns(chunk)]
+                if (chunk, c) == (0, 0):
+                    nc.vector.tensor_scalar_mul(target, source, -1.0)
+                else:
+                    nc.scalar.mul(target, source, -1.0)
 
-        def paired(chunk, m):
-            return (chunk, m) == (0, 0)
+        def in_psum(m):
+            return m == 0
 
         def products(chunk, neighbours):
             banks = {k: [free_banks.pop(0) for m in range(BLOCKS)] for k in neighbours}
@@ -85,43 +90,58 @@ def tile_pctransformer_kernel(tc, x, w_knn, b_knn, offs, out):
                     nc.scalar.mul(d_bf[:], d_f32[:], -1.0 if negated else 1.0)
                     for m in range(BLOCKS):
                         weights = w_diff[:, c, m * P : (m + 1) * P]
-                        stays_open = k == 0 and paired(chunk, m)
-                        is_open = negated and paired(chunk, m)
+                        stays_open = (chunk, k) == (0, 0) and in_psum(m)
                         nc.tensor.matmul(
                             banks[k][m][:],
                             weights,
                             d_bf[:],
-                            start=(c == 0 and not is_open),
+                            start=(c == 0 and not negated),
                             stop=(c == BLOCKS - 1 and not stays_open),
                         )
-                        if stays_open:
+                        if (chunk, k) == (0, 0):
                             nc.tensor.matmul(banks[1][m][:], weights, d_bf[:], start=(c == 0), stop=False)
             return banks
 
-        first_bank = {}
+        first = {m: held.tile([P, PIECE], F32, name=f"first_{m}") for m in range(1, BLOCKS)}
+        pair = {m: held.tile([P, PIECE], F32, name=f"pair_{m}") for m in range(1, BLOCKS)}
+        pair_bank = {}
+
+        def take_first(banks):
+            for m in range(BLOCKS):
+                if in_psum(m):
+                    pair_bank[m] = banks[m]
+                else:
+                    nc.scalar.copy(first[m][:], banks[m][:])
+                    free_banks.append(banks[m])
+
+        def pair_up(banks):
+            for m in range(BLOCKS):
+                gain = work.tile([P, PIECE], F32, name="gain")
+                nc.scalar.activation(gain[:], banks[m][:], RELU, scale=-1.0)
+                if in_psum(m):
+                    nc.tensor.matmul(pair_bank[m][:], identity[:], gain[:], start=False, stop=True)
+                else:
+                    nc.gpsimd.tensor_tensor(pair[m][:], first[m][:], gain[:], ADD)
+                free_banks.append(banks[m])
+
+        def merge_pair(m):
+            source = pair_bank[m] if in_psum(m) else pair[m]
+            nc.vector.tensor_tensor(best[0][m][:], source[:], best[0][m][:], MAX)
+            if in_psum(m):
+                free_banks.append(source)
 
         def fold(chunk, k, banks):
             for m in range(BLOCKS):
-                bank, running = banks[m], best[chunk][m]
-                if paired(chunk, m) and k < 3:
-                    if k == 0:
-                        first_bank[m] = bank
-                        continue
-                    if k == 1:
-                        gain = work.tile([P, PIECE], F32, name="gain")
-                        nc.scalar.activation(gain[:], bank[:], RELU, scale=-1.0)
-                        nc.tensor.matmul(first_bank[m][:], identity[:], gain[:], start=False, stop=True)
-                        nc.scalar.copy(running[:], first_bank[m][:])
-                        free_banks.append(first_bank[m])
-                    if k == 2:
-                        nc.vector.tensor_tensor(running[:], bank[:], running[:], MAX)
-                elif k == 0:
-                    nc.scalar.copy(running[:], bank[:])
-                elif k == 1 and chunk == 0:
-                    nc.vector.scalar_tensor_tensor(running[:], bank[:], -1.0, running[:], MULT, MAX)
+                if k == FIRST_FOLDED[chunk]:
+                    nc.scalar.copy(best[chunk][m][:], banks[m][:])
                 else:
-                    nc.vector.tensor_tensor(running[:], bank[:], running[:], MAX)
-                free_banks.append(bank)
+                    nc.vector.tensor_tensor(best[chunk][m][:], banks[m][:], best[chunk][m][:], MAX)
+            free_banks.extend(banks)
+            if (chunk, k) == (0, 2):
+                merge_pair(0)
+            if (chunk, k) == (0, 3):
+                for m in range(1, BLOCKS):
+                    merge_pair(m)
 
 
         def round_own(chunk):
@@ -174,29 +194,29 @@ def tile_pctransformer_kernel(tc, x, w_knn, b_knn, offs, out):
 
         negate(0)
         round_own(LAST)
-        take_out(1, own_term(LAST, 1, closed=True))
-        banks = products(0, (0, 1))
-        fold(0, 0, banks[0])
-        unfolded = (0, 1, banks[1])
-        bias_low = held.tile([P, BLOCKS], F32, name="bias_low")
-        bias_high = held.tile([P, BLOCKS], F32, name="bias_high")
-        nc.scalar.mul(bias_low[:], bias[:], SLOPE)
-        nc.scalar.mul(bias_high[:], bias[:], 1.0 - SLOPE)
+        take_out(2, own_term(LAST, 2, closed=True))
+        paired = products(0, (0, 1))
+        take_first(paired[0])
+        unfolded = None
         for chunk in range(CHUNKS):
             if chunk > 0:
                 negate(chunk)
-            for k in range(2 if chunk == 0 else 0, K):
-                banks = products(chunk, (k,))
-                fold(*unfolded)
-                if (chunk, k) == (0, 2):
-                    round_own(0)
+            for k in range(FIRST_FOLDED[chunk], K):
+                banks = products(chunk, (k,))[k]
+                if unfolded is None:
+                    pair_up(paired[1])
+                    bias_low = held.tile([P, BLOCKS], F32, name="bias_low")
+                    bias_high = held.tile([P, BLOCKS], F32, name="bias_high")
+                    nc.scalar.mul(bias_low[:], bias[:], SLOPE)
+                    nc.scalar.mul(bias_high[:], bias[:], 1.0 - SLOPE)
+                else:
+                    fold(*unfolded)
+                if (chunk, k) == (0, K - 1):
+                    take_out(1, own_term(LAST, 1, closed=True))
                 if chunk == LAST and k == 0:
-                    finish_without_vector(0, 0)
-                    finish_without_vector(0, 1)
-                if chunk == LAST and k == 1:
-                    finish_without_vector(0, 2)
-                if (chunk, k) == (LAST, K - 1):
-                    take_out(2, own_term(LAST, 2, closed=True))
-                unfolded = (chunk, k, banks[k])
+                    round_own(0)
+                if chunk == LAST and k < BLOCKS:
+                    finish_without_vector(0, k)
+                unfolded = (chunk, k, banks)
         fold(*unfolded)
         finish_last_chunk()

@@ -40,8 +40,7 @@ def tile_pctransformer_kernel(tc, x, w_knn, b_knn, offs, out):
 
         x_f32 = [held.tile([P, S], F32, name=f"x_f32_{c}") for c in range(BLOCKS)]
         offsets = held.tile([P, N // 16], U16, name="offsets")
-        for chunk in range(CHUNKS):
-            nc.sync.dma_start(x_f32[0][:, columns(chunk)], x[0:P, columns(chunk)])
+        nc.sync.dma_start(x_f32[0][:], x[0:P, :])
         nc.sync.dma_start(offsets[:], offs)
         for c in range(1, BLOCKS):
             nc.sync.dma_start(x_f32[c][:], x[c * P : (c + 1) * P, :])

import concourse.mybir as mybir
from concourse.masks import make_identity

F32 = mybir.dt.float32
BF16 = mybir.dt.bfloat16
U16 = mybir.dt.uint16
ADD = mybir.AluOpType.add
MULT = mybir.AluOpType.mult
MAX = mybir.AluOpType.max
IDENTITY = mybir.ActivationFunctionType.Identity
RELU = mybir.ActivationFunctionType.Relu

P = 128
C = 384
S = 1024
K = 4
N = K * S
SLOPE = 0.2
BLOCKS = C // P
PIECE = 512
CHUNKS = S // PIECE
BANKS = 8
LAST = CHUNKS - 1
FIRST_FOLDED = (2, 0)

FLOPS = 2 * C * C * (N + S)


def tile_pctransformer_kernel(tc, x, w_knn, b_knn, offs, out):
    nc = tc.nc
    with (
        tc.tile_pool(name="held", bufs=1) as held,
        tc.tile_pool(name="diff", bufs=6) as diff,
        tc.tile_pool(name="moving", bufs=4) as moving,
        tc.tile_pool(name="work", bufs=CHUNKS * BLOCKS) as work,
        tc.psum_pool(name="psum", bufs=1) as psum,
    ):
        def columns(chunk):
            return slice(chunk * PIECE, (chunk + 1) * PIECE)

        x_f32 = [held.tile([P, S], F32, name=f"x_f32_{c}") for c in range(BLOCKS)]
        offsets = held.tile([P, N // 16], U16, name="offsets")
        nc.sync.dma_start(x_f32[0][:], x[0:P, :])
        nc.sync.dma_start(offsets[:], offs)
        for c in range(1, BLOCKS):
            nc.sync.dma_start(x_f32[c][:], x[c * P : (c + 1) * P, :])
        w_diff = held.tile([P, BLOCKS, C], BF16, name="w_diff")
        w_own = held.tile([P, BLOCKS, C], BF16, name="w_own")
        nc.sync.dma_start(w_own[:], w_knn[C : 2 * C, :].rearrange("(c p) m -> p c m", p=P))
        nc.sync.dma_start(w_diff[:], w_knn[0:C, :].rearrange("(c p) m -> p c m", p=P))
        bias = held.tile([P, BLOCKS], F32, name="bias")
        with nc.allow_non_contiguous_dma(reason="384 bias values, one to a partition"):
            nc.sync.dma_start(bias[:], b_knn.rearrange("(m p) o -> p (m o)", p=P))
        identity = held.tile([P, P], F32, name="identity")
        make_identity(nc, identity[:])

        x_neg = [held.tile([P, S], F32, name=f"x_neg_{c}") for c in range(BLOCKS)]
        x_bf = [held.tile([P, S], BF16, name=f"x_bf_{c}") for c in range(BLOCKS)]
        best = [[held.tile([P, PIECE], F32, name=f"best{chunk}_{m}") for m in range(BLOCKS)] for chunk in range(CHUNKS)]
        v_max = [held.tile([P, PIECE], F32, name=f"v_max_{m}") for m in range(BLOCKS)]

        free_banks = [psum.tile([P, PIECE], F32, name=f"bank{b}") for b in range(BANKS)]

        def negate(chunk):
            for c in range(BLOCKS):
                source, target = x_f32[c][:, columns(chunk)], x_neg[c][:, columns(chunk)]
                if (chunk, c) == (0, 0):
                    nc.vector.tensor_scalar_mul(target, source, -1.0)
                else:
                    nc.scalar.mul(target, source, -1.0)

        def in_psum(m):
            return m == 0

        def products(chunk, neighbours):
            banks = {k: [free_banks.pop(0) for m in range(BLOCKS)] for k in neighbours}
            for c in range(BLOCKS):
                for k in neighbours:
                    negated = (chunk, k) == (0, 1)
                    entry = (k * S + chunk * PIECE) // 16
                    d_f32 = diff.tile([P, PIECE], F32, name="d_f32")
                    nc.vector.tensor_tensor(
                        d_f32[:],
                        x_f32[c][:].indirect(offsets[:, entry : entry + PIECE // 16]),
                        x_neg[c][:, columns(chunk)],
                        ADD,
                    )
                    d_bf = moving.tile([P, PIECE], BF16, name="d_bf")
                    nc.scalar.mul(d_bf[:], d_f32[:], -1.0 if negated else 1.0)
                    for m in range(BLOCKS):
                        weights = w_diff[:, c, m * P : (m + 1) * P]
                        stays_open = (chunk, k) == (0, 0) and in_psum(m)
                        nc.tensor.matmul(
                            banks[k][m][:],
                            weights,
                            d_bf[:],
                            start=(c == 0 and not negated),
                            stop=(c == BLOCKS - 1 and not stays_open),
                        )
                        if (chunk, k) == (0, 0):
                            nc.tensor.matmul(banks[1][m][:], weights, d_bf[:], start=(c == 0), stop=False)
            return banks

        first = {m: held.tile([P, PIECE], F32, name=f"first_{m}") for m in range(1, BLOCKS)}
        pair = {m: held.tile([P, PIECE], F32, name=f"pair_{m}") for m in range(1, BLOCKS)}
        pair_bank = {}

        def take_first(banks):
            for m in range(BLOCKS):
                if in_psum(m):
                    pair_bank[m] = banks[m]
                else:
                    nc.scalar.copy(first[m][:], banks[m][:])
                    free_banks.append(banks[m])

        def pair_up(banks):
            for m in range(BLOCKS):
                gain = work.tile([P, PIECE], F32, name="gain")
                nc.scalar.activation(gain[:], banks[m][:], RELU, scale=-1.0)
                if in_psum(m):
                    nc.tensor.matmul(pair_bank[m][:], identity[:], gain[:], start=False, stop=True)
                else:
                    nc.gpsimd.tensor_tensor(pair[m][:], first[m][:], gain[:], ADD)
                free_banks.append(banks[m])

        def merge_pair(m):
            source = pair_bank[m] if in_psum(m) else pair[m]
            nc.vector.tensor_tensor(best[0][m][:], source[:], best[0][m][:], MAX)
            if in_psum(m):
                free_banks.append(source)

        def fold(chunk, k, banks):
            for m in range(BLOCKS):
                if k == FIRST_FOLDED[chunk]:
                    nc.scalar.copy(best[chunk][m][:], banks[m][:])
                else:
                    nc.vector.tensor_tensor(best[chunk][m][:], banks[m][:], best[chunk][m][:], MAX)
            free_banks.extend(banks)
            if (chunk, k) == (0, 2):
                merge_pair(0)
            if (chunk, k) == (0, 3):
                for m in range(1, BLOCKS):
                    merge_pair(m)


        def round_own(chunk):
            for c in range(BLOCKS):
                nc.scalar.copy(x_bf[c][:, columns(chunk)], x_f32[c][:, columns(chunk)])

        def own_term(chunk, m, closed):
            bank = free_banks.pop(0)
            for c in range(BLOCKS):
                nc.tensor.matmul(
                    bank[:],
                    w_own[:, c, m * P : (m + 1) * P],
                    x_bf[c][:, columns(chunk)],
                    start=(c == 0),
                    stop=(closed and c == BLOCKS - 1),
                )
            return bank

        def sum_in_psum(chunk, m):
            bank = own_term(chunk, m, closed=False)
            nc.tensor.matmul(bank[:], identity[:], best[chunk][m][:], start=False, stop=True)
            return bank

        def take_out(m, bank):
            nc.scalar.activation(v_max[m][:], bank[:], IDENTITY, bias=bias[:, m : m + 1])
            free_banks.append(bank)

        def finish_without_vector(chunk, m):
            bank = sum_in_psum(chunk, m)
            low = work.tile([P, PIECE], F32, name="low")
            high = work.tile([P, PIECE], F32, name="high")
            nc.scalar.activation(low[:], bank[:], IDENTITY, bias=bias_low[:, m : m + 1], scale=SLOPE)
            nc.scalar.activation(high[:], bank[:], RELU, bias=bias_high[:, m : m + 1], scale=1.0 - SLOPE)
            free_banks.append(bank)
            result = work.tile([P, PIECE], F32, name="result")
            nc.gpsimd.tensor_tensor(result[:], low[:], high[:], ADD)
            nc.sync.dma_start(out[m * P : (m + 1) * P, columns(chunk)], result[:])

        def finish_last_chunk():
            take_out(0, sum_in_psum(LAST, 0))
            for m in range(1, BLOCKS):
                nc.vector.tensor_tensor(v_max[m][:], best[LAST][m][:], v_max[m][:], ADD)
            for m in (1, 2, 0):
                for half in range(0, PIECE, PIECE // 2):
                    part = slice(half, half + PIECE // 2)
                    result = work.tile([P, PIECE // 2], F32, name="half_result")
                    nc.vector.scalar_tensor_tensor(result[:], v_max[m][:, part], SLOPE, v_max[m][:, part], MULT, MAX)
                    left = LAST * PIECE + half
                    nc.sync.dma_start(out[m * P : (m + 1) * P, left : left + PIECE // 2], result[:])

        negate(0)
        round_own(LAST)
        take_out(2, own_term(LAST, 2, closed=True))
        paired = products(0, (0, 1))
        take_first(paired[0])
        unfolded = None
        for chunk in range(CHUNKS):
            if chunk > 0:
                negate(chunk)
            for k in range(FIRST_FOLDED[chunk], K):
                banks = products(chunk, (k,))[k]
                if unfolded is None:
                    pair_up(paired[1])
                    bias_low = held.tile([P, BLOCKS], F32, name="bias_low")
                    bias_high = held.tile([P, BLOCKS], F32, name="bias_high")
                    nc.scalar.mul(bias_low[:], bias[:], SLOPE)
                    nc.scalar.mul(bias_high[:], bias[:], 1.0 - SLOPE)
                else:
                    fold(*unfolded)
                if (chunk, k) == (0, K - 1):
                    take_out(1, own_term(LAST, 1, closed=True))
                if chunk == LAST and k == 0:
                    round_own(0)
                if chunk == LAST and k < BLOCKS:
                    finish_without_vector(0, k)
                unfolded = (chunk, k, banks)
        fold(*unfolded)
        finish_last_chunk()
